import numpy as np
import ml_dtypes


def mxq(x, axis, fmt="e4m3"):
    dtype, down = {"e4m3": (ml_dtypes.float8_e4m3fn, 7), "e5m2": (ml_dtypes.float8_e5m2, 14)}[fmt]
    v = np.moveaxis(np.asarray(x, np.float32).astype(ml_dtypes.bfloat16).astype(np.float64), axis, -1)
    blocks = v.reshape(v.shape[:-1] + (-1, 32))
    amax = np.abs(blocks).max(-1, keepdims=True)
    byte = np.maximum(np.where(amax > 0, np.frexp(amax)[1] - 1 + 127, 0) - down, 1)
    scale = np.exp2(byte - 127.0)
    codes = (blocks / scale).astype(np.float32).astype(dtype).astype(np.float64)
    return np.moveaxis((codes * scale).reshape(v.shape), -1, axis)


WIDE = False


def mx_kscale(k):
    if not WIDE:
        return np.ones(k)
    levels = np.array([10, -10, 5, -5, 0])
    if k % 512:
        return np.exp2(np.random.permutation(np.resize(levels, k // 32))).repeat(32)
    a = np.empty((k // 512, 16))
    for p in range(k // 512):
        a[p, :8] = np.random.permutation(np.resize(levels, 8))
        for g in range(8):
            far = levels[np.abs(levels - a[p, g]) >= 10]
            a[p, g + 8] = far[np.random.randint(len(far))]
    return np.exp2(a.ravel()).repeat(32)


BF16 = ml_dtypes.bfloat16


def bf(x):
    return np.asarray(x, np.float32).astype(BF16)


def f64(x):
    return np.asarray(x).astype(np.float64)


E2M1 = np.array([0.0, 0.5, 1.0, 1.5, 2.0, 3.0, 4.0, 6.0, -0.0, -0.5, -1.0, -1.5, -2.0, -3.0, -4.0, -6.0])


def pack_weight(w, fmt):
    k, n = w.shape
    w = f64(bf(w)).reshape(k // 32, 32, n)
    amax = np.abs(w).max(1)
    if fmt == "e4m3":
        byte = np.frexp(amax)[1] - 1 + 127 - 7
    else:
        mant, ex = np.frexp(amax / 6.0)
        byte = np.where(mant > 0.5, ex, ex - 1) + 127
    byte = np.clip(np.where(amax > 0, byte, 1), 1, 254)
    scaled = (w * np.exp2(127.0 - byte)[:, None, :]).reshape(k, n).astype(np.float32)
    by_word = np.ascontiguousarray(scaled.reshape(k // 512, 128, 4, n).transpose(0, 1, 3, 2))
    if fmt == "e4m3":
        words = by_word.astype(ml_dtypes.float8_e4m3fn).view(np.uint8)
    else:
        c = by_word.astype(ml_dtypes.float4_e2m1fn).view(np.uint8) & 0xF
        words = c[..., 0::2] | (c[..., 1::2] << 4)
    return np.ascontiguousarray(words), np.ascontiguousarray(byte.astype(np.uint8).reshape(k // 512, 16, n))


def unpack_weight(words, scales, fmt):
    g, p, n, _ = words.shape
    if fmt == "e4m3":
        vals = np.ascontiguousarray(words).view(ml_dtypes.float8_e4m3fn).astype(np.float64)
    else:
        nib = np.empty((g, p, n, 4), np.uint8)
        nib[..., 0::2] = words & 0xF
        nib[..., 1::2] = words >> 4
        vals = E2M1[nib]
    vals = vals * np.repeat(np.exp2(scales.astype(np.float64) - 127.0), 8, axis=1)[..., None]
    return vals.transpose(0, 1, 3, 2).reshape(g * 512, n)
def pack4(w):
    words, scales = pack_weight(w, "e2m1")
    return words.reshape(words.shape[0], 128, -1), scales


def unpack4(words, scales):
    return unpack_weight(words.reshape(words.shape[0], 128, -1, 2), scales, "e2m1")


B, L, D = 3, 512, 512
SIG = 2.0


def draw0():
    s, t = mx_kscale(D), mx_kscale(D)
    x1 = bf(np.random.standard_normal((B, L, D)) * s)
    words, scales = pack4(np.random.standard_normal((D, D)) * SIG / D / s[:, None] * t)
    return {"x1": x1,
            "bi_linear_w_words": words,
            "bi_linear_w_scales": scales,
            "x2": bf(np.random.standard_normal((B, L, D)) / t)}


def core(x1, bi_linear_w_words, bi_linear_w_scales, x2):
    h = mxq(f64(x1), 2, "e4m3") @ unpack4(bi_linear_w_words, bi_linear_w_scales)
    return mxq(h, 2, "e4m3") @ mxq(f64(x2), 2, "e4m3").transpose(0, 2, 1)


def e4m3fn_bytes(y):
    return np.clip(np.asarray(y, np.float64), -448.0, 448.0).astype(np.float32).astype(ml_dtypes.float8_e4m3fn).view(np.uint8)


def e4m3fn_values(b):
    return np.asarray(b, np.uint8).view(ml_dtypes.float8_e4m3fn).astype(np.float64)


def setup_inputs():
    d = draw0()
    x0 = np.asarray(d['x2']).astype(np.float64)
    s = (np.max(np.abs(x0), axis=(0, 1), keepdims=True) / 448.0).astype(np.float32)
    out = {}
    for k, v in d.items():
        if k == 'x2':
            out['x2_bytes'] = e4m3fn_bytes(x0 / s.astype(np.float64))
            out['x2_scale'] = s
        else:
            out[k] = v
    return out


def reference(x1, bi_linear_w_words, bi_linear_w_scales, x2_bytes, x2_scale):
    return core(x1, bi_linear_w_words, bi_linear_w_scales, e4m3fn_values(x2_bytes) * x2_scale.astype(np.float64))

@@ -1,0 +1,226 @@
+from contextlib import ExitStack
+
+import concourse.mybir as mybir
+from concourse.masks import make_identity
+
+B, L, D = 3, 512, 512
+P = 128
+FLOPS = 2 * 2 * B * L * L * D
+
+F32 = mybir.dt.float32
+BF16 = mybir.dt.bfloat16
+I32 = mybir.dt.int32
+U32 = mybir.dt.uint32
+U8 = mybir.dt.uint8
+E4M3 = mybir.dt.float8_e4m3fn
+FP8X4 = mybir.dt.float8_e4m3fn_x4
+FP4X4 = mybir.dt.float4_e2m1fn_x4
+MULT = mybir.AluOpType.mult
+
+HALVES = 2 * B
+ON_VECTOR = (("HC0", 3), ("HC0", 4), ("HC1", 5), ("OC0", 3), ("OC1", 0), ("OC1", 5))
+HROWS = 256
+
+
+def tile_coattentionandcombine_pa_w4_kernel(tc, x1, w_words, w_scales, x2_bytes, x2_scale, out):
+    nc = tc.nc
+    with ExitStack() as ctx:
+        keep = ctx.enter_context(tc.tile_pool(name="keep", bufs=1))
+        work = ctx.enter_context(tc.tile_pool(name="work", bufs=6))
+        psum = ctx.enter_context(tc.psum_pool(name="psum", bufs=2))
+        ctx.enter_context(tc.manual_schedule())
+
+        x1_raw = [keep.tile([P, 2, D], BF16, name="x1_raw%d" % i) for i in range(HALVES)]
+        x2_codes_in = [keep.tile([P, 2 * D], U8, name="x2_in%d" % i) for i in range(HALVES)]
+        x2_words = [keep.tile([P, L], U32, name="x2_words%d" % b, align_bytes=64) for b in range(B)]
+        x2_planes = [keep.tile([P, L], U8, name="x2_planes%d" % b, align_bytes=64) for b in range(B)]
+        scale_col = keep.tile([P, 4], F32, name="scale_col")
+        scale_row = keep.tile([P, 2, D], F32, name="scale_row")
+        w_raw = keep.tile([P, 2 * D], U8, name="w_raw", align_bytes=64)
+        w_raw_plane = keep.tile([P, D], U8, name="w_raw_plane", align_bytes=64)
+        w = keep.tile([P, 2 * D], U8, name="w", align_bytes=64)
+        w_plane = keep.tile([P, D], U8, name="w_plane", align_bytes=64)
+        ident = keep.tile([P, P], F32, name="ident")
+        warm = keep.tile([P, 2], F32, name="warm")
+
+        x1_view = x1.rearrange("b (p c) k -> b p c k", c=4)
+        x2_view = x2_bytes.rearrange("b (p c) k -> b p (c k)", c=4)
+        out_view = out.rearrange("b (p c) n -> b p c n", c=4)
+
+        def load_x1(i):
+            b, j = divmod(i, 2)
+            nc.sync.dma_start(out=x1_raw[i][:], in_=x1_view[b, :, 2 * j : 2 * j + 2, :])
+
+        def load_x2(i):
+            b, j = divmod(i, 2)
+            nc.sync.dma_start(out=x2_codes_in[i][:], in_=x2_view[b, :, 2 * D * j : 2 * D * (j + 1)])
+
+        nc.vector.memset(w_raw_plane[:].bitcast(I32), 0)
+        nc.vector.memset(warm[:], 0.0)
+        nc.scalar.dma_start(out=scale_col[:], in_=x2_scale.rearrange("a o (p t) -> p (a o t)", t=4))
+        nc.scalar.copy(out=warm[:, 0:1], in_=warm[:, 1:2])
+        load_x1(0)
+        load_x2(0)
+        nc.sync.dma_start(out=w_raw[:].bitcast(I32), in_=w_words.rearrange("g p n -> p (g n)").bitcast(I32))
+        load_x1(1)
+        for q in range(4):
+            nc.sync.dma_start(out=w_raw_plane[32 * q : 32 * q + 4, :].bitcast(I32), in_=w_scales[0, 4 * q : 4 * q + 4, :].bitcast(I32))
+        load_x2(1)
+        load_x1(2)
+        load_x1(3)
+        load_x2(2)
+        load_x2(3)
+        load_x1(4)
+        load_x1(5)
+        load_x2(4)
+        load_x2(5)
+        make_identity(nc, ident[:])
+
+        spread = psum.tile([P, 4, P], F32, name="spread", tag="x2_turned")
+        for t in range(4):
+            nc.tensor.transpose(spread[:, t, :], scale_col[:, t : t + 1].to_broadcast([P, P]), ident[:])
+        nc.scalar.copy(out=scale_row[:, 0, :].rearrange("p (n t) -> p n t", t=4), in_=spread[:].rearrange("p t n -> p n t"))
+
+        turned, k_first, x1_q, h_acc, h, h_q, x2_rows, sums = {}, {}, {}, {}, {}, {}, {}, {}
+
+        def fits(name, i):
+            return nc.vector.tensor_copy if (name, i) in ON_VECTOR else nc.scalar.copy
+
+        def turn(name, i, rows):
+            words = rows.bitcast(F32)
+            acc = psum.tile([P, 2, 2, P], F32, name=name + "_turned", tag=name + "_turned")
+            for c in range(2):
+                for u in range(2):
+                    nc.tensor.transpose(acc[:, u, c, :], words[:, 256 * c + u : 256 * (c + 1) : 2], ident[:])
+            turned[name, i] = acc
+
+        def interleave(name, i, stage):
+            out_tile = work.tile([P, HROWS * 4], BF16, name=name + "_k", tag=name + "_k", align_bytes=64)
+            fits(stage, i)(
+                out=out_tile[:].bitcast(F32).rearrange("p (r u) -> p r u", u=2),
+                in_=turned[name, i][:].rearrange("p u c r -> p (c r) u"),
+            )
+            k_first[name, i] = out_tile
+
+        def quantize(rows, name):
+            words = work.tile([P, HROWS], U32, name=name + "_w", tag=name + "_w", align_bytes=64)
+            plane = work.tile([P, HROWS], U8, name=name + "_s", tag=name + "_s", align_bytes=64)
+            nc.vector.quantize_mx(out=words[:].bitcast(FP8X4), scales=plane[:], in_=rows[:])
+            return words, plane
+
+        def stage_W(i):
+            if i == 0:
+                nc.vector.tensor_copy(out=w[:].rearrange("p (t m e) -> p t m e", t=4, e=2), in_=w_raw[:].rearrange("p (m t e) -> p t m e", t=4, e=2))
+                nc.gpsimd.tensor_copy(out=w_plane[:].rearrange("p (t m) -> p t m", t=4), in_=w_raw_plane[:].rearrange("p (m t) -> p t m", t=4))
+                nc.vector.tensor_copy(out=scale_row[:, 1, :], in_=scale_row[:, 0, :])
+
+        def stage_T1(i):
+            turn("x1", i, x1_raw[i][:].rearrange("p c k -> p (c k)"))
+
+        def stage_C1(i):
+            interleave("x1", i, "C1")
+
+        def stage_Q1(i):
+            x1_q[i] = quantize(k_first["x1", i], "x1")
+
+        def stage_P(i):
+            rows = work.tile([P, 2 * D], BF16, name="x2_rows", tag="x2_rows")
+            nc.vector.tensor_tensor(out=rows[:], in0=x2_codes_in[i][:].bitcast(E4M3), in1=scale_row[:].rearrange("p c k -> p (c k)"), op=MULT)
+            x2_rows[i] = rows
+
+        def stage_T2(i):
+            turn("x2", i, x2_rows[i][:])
+
+        def stage_C2(i):
+            interleave("x2", i, "C2")
+
+        def stage_Q2(i):
+            b, j = divmod(i, 2)
+            cols = slice(HROWS * j, HROWS * (j + 1))
+            nc.vector.quantize_mx(out=x2_words[b][:, cols].bitcast(FP8X4), scales=x2_planes[b][:, cols], in_=k_first["x2", i][:])
+
+        def stage_H(i):
+            words, plane = x1_q[i]
+            for c in range(2):
+                rows = slice(P * c, P * (c + 1))
+                acc = psum.tile([P, 4, P], F32, name="h_acc", tag="h_acc")
+                for t in range(4):
+                    nc.tensor.matmul_mx(
+                        out=acc[:, t, :],
+                        lhsT=w[:, 256 * t : 256 * (t + 1)].bitcast(FP4X4),
+                        lhsT_scale=w_plane[:, P * t : P * (t + 1)],
+                        rhs=words[:, rows].bitcast(FP8X4),
+                        rhs_scale=plane[:, rows],
+                        start=True,
+                        stop=True,
+                    )
+                h_acc[i, c] = acc
+
+        def h_out(i, c, stage):
+            if c == 0:
+                h_tile = work.tile([P, HROWS * 4], BF16, name="h", tag="h", align_bytes=64)
+                h[i] = h_tile
+            fits(stage, i)(
+                out=h[i][:, 512 * c : 512 * (c + 1)].rearrange("p (r t) -> p r t", t=4),
+                in_=h_acc[i, c][:].rearrange("p t r -> p r t"),
+            )
+
+        def stage_HC0(i):
+            h_out(i, 0, "HC0")
+
+        def stage_HC1(i):
+            h_out(i, 1, "HC1")
+
+        def stage_HQ(i):
+            h_q[i] = quantize(h[i], "h")
+
+        def stage_O(i):
+            b = i // 2
+            words, plane = h_q[i]
+            for c in range(2):
+                rows = slice(P * c, P * (c + 1))
+                acc = psum.tile([P, L], F32, name="sim_acc", tag="sim_acc")
+                nc.tensor.matmul_mx(
+                    out=acc[:],
+                    lhsT=words[:, rows].bitcast(FP8X4),
+                    lhsT_scale=plane[:, rows],
+                    rhs=x2_words[b][:].bitcast(FP8X4),
+                    rhs_scale=x2_planes[b][:],
+                    start=True,
+                    stop=True,
+                )
+                sums[i, c] = acc
+
+        def sim_out(i, c, stage):
+            b, j = divmod(i, 2)
+            result = work.tile([P, L], F32, name="result", tag="result", bufs=12)
+            fits(stage, i)(out=result[:].rearrange("p (m c) -> p m c", c=4), in_=sums[i, c][:].rearrange("p (c m) -> p m c", c=4))
+            nc.sync.dma_start(out=out_view[b, :, 2 * j + c, :], in_=result[:])
+
+        def stage_OC0(i):
+            sim_out(i, 0, "OC0")
+
+        def stage_OC1(i):
+            sim_out(i, 1, "OC1")
+
+        order = (
+            (stage_C2, 3),
+            (stage_P, 1),
+            (stage_H, 4),
+            (stage_HC0, 4),
+            (stage_T1, 0),
+            (stage_O, 5),
+            (stage_T2, 2),
+            (stage_HC1, 4),
+            (stage_OC0, 5),
+            (stage_Q2, 3),
+            (stage_OC1, 5),
+            (stage_C1, 0),
+            (stage_W, 0),
+            (stage_HQ, 4),
+            (stage_Q1, 2),
+        )
+        for step in range(HALVES + max(lag for stage, lag in order)):
+            for stage, lag in order:
+                if 0 <= step - lag < HALVES:
+                    stage(step - lag)

@@ -18,7 +18,8 @@ FP4X4 = mybir.dt.float4_e2m1fn_x4
 MULT = mybir.AluOpType.mult
 
 HALVES = 2 * B
-ON_VECTOR = (("HC0", 3), ("HC0", 4), ("HC1", 5), ("OC0", 3), ("OC1", 0), ("OC1", 5))
+BANKS = {"x1": 2, "x2": 1, "h": 2, "sim": 3}
+ON_VECTOR = (("C2", 3), ("HC1", 4), ("HC1", 5), ("OC1", 1), ("OC1", 2), ("OC1", 4))
 HROWS = 256
 
 
@@ -30,12 +31,12 @@ def tile_coattentionandcombine_pa_w4_kernel(tc, x1, w_words, w_scales, x2_bytes,
         psum = ctx.enter_context(tc.psum_pool(name="psum", bufs=2))
         ctx.enter_context(tc.manual_schedule())
 
-        x1_raw = [keep.tile([P, 2, D], BF16, name="x1_raw%d" % i) for i in range(HALVES)]
-        x2_codes_in = [keep.tile([P, 2 * D], U8, name="x2_in%d" % i) for i in range(HALVES)]
+        x1_raw = [keep.tile([P, 4 * D], BF16, name="x1_raw%d" % b) for b in range(B)]
+        x2_raw = [keep.tile([P, 4 * D], U8, name="x2_raw%d" % b) for b in range(B)]
         x2_words = [keep.tile([P, L], U32, name="x2_words%d" % b, align_bytes=64) for b in range(B)]
         x2_planes = [keep.tile([P, L], U8, name="x2_planes%d" % b, align_bytes=64) for b in range(B)]
         scale_col = keep.tile([P, 4], F32, name="scale_col")
-        scale_row = keep.tile([P, 2, D], F32, name="scale_row")
+        scale_row = keep.tile([P, D], F32, name="scale_row")
         w_raw = keep.tile([P, 2 * D], U8, name="w_raw", align_bytes=64)
         w_raw_plane = keep.tile([P, D], U8, name="w_raw_plane", align_bytes=64)
         w = keep.tile([P, 2 * D], U8, name="w", align_bytes=64)
@@ -43,43 +44,39 @@ def tile_coattentionandcombine_pa_w4_kernel(tc, x1, w_words, w_scales, x2_bytes,
         ident = keep.tile([P, P], F32, name="ident")
         warm = keep.tile([P, 2], F32, name="warm")
 
-        x1_view = x1.rearrange("b (p c) k -> b p c k", c=4)
+        x1_view = x1.rearrange("b (p c) k -> b p (c k)", c=4)
         x2_view = x2_bytes.rearrange("b (p c) k -> b p (c k)", c=4)
         out_view = out.rearrange("b (p c) n -> b p c n", c=4)
 
-        def load_x1(i):
-            b, j = divmod(i, 2)
-            nc.sync.dma_start(out=x1_raw[i][:], in_=x1_view[b, :, 2 * j : 2 * j + 2, :])
+        def load(tiles, view, b, halves):
+            cols = slice(2 * D * halves[0], 2 * D * (halves[-1] + 1))
+            nc.sync.dma_start(out=tiles[b][:, cols], in_=view[b, :, cols])
 
-        def load_x2(i):
+        def half(tiles, i):
             b, j = divmod(i, 2)
-            nc.sync.dma_start(out=x2_codes_in[i][:], in_=x2_view[b, :, 2 * D * j : 2 * D * (j + 1)])
+            return tiles[b][:, 2 * D * j : 2 * D * (j + 1)]
 
         nc.vector.memset(w_raw_plane[:].bitcast(I32), 0)
         nc.vector.memset(warm[:], 0.0)
         nc.scalar.dma_start(out=scale_col[:], in_=x2_scale.rearrange("a o (p t) -> p (a o t)", t=4))
         nc.scalar.copy(out=warm[:, 0:1], in_=warm[:, 1:2])
-        load_x1(0)
-        load_x2(0)
         nc.sync.dma_start(out=w_raw[:].bitcast(I32), in_=w_words.rearrange("g p n -> p (g n)").bitcast(I32))
-        load_x1(1)
+        load(x2_raw, x2_view, 0, (0,))
+        load(x1_raw, x1_view, 0, (0,))
+        load(x1_raw, x1_view, 0, (1,))
         for q in range(4):
             nc.sync.dma_start(out=w_raw_plane[32 * q : 32 * q + 4, :].bitcast(I32), in_=w_scales[0, 4 * q : 4 * q + 4, :].bitcast(I32))
-        load_x2(1)
-        load_x1(2)
-        load_x1(3)
-        load_x2(2)
-        load_x2(3)
-        load_x1(4)
-        load_x1(5)
-        load_x2(4)
-        load_x2(5)
+        load(x2_raw, x2_view, 0, (1,))
+        load(x1_raw, x1_view, 1, (0, 1))
+        load(x2_raw, x2_view, 1, (0, 1))
+        load(x1_raw, x1_view, 2, (0, 1))
+        load(x2_raw, x2_view, 2, (0, 1))
         make_identity(nc, ident[:])
 
-        spread = psum.tile([P, 4, P], F32, name="spread", tag="x2_turned")
+        spread = psum.tile([P, 4, P], F32, name="spread", tag="x2_turned", bufs=BANKS["x2"])
         for t in range(4):
             nc.tensor.transpose(spread[:, t, :], scale_col[:, t : t + 1].to_broadcast([P, P]), ident[:])
-        nc.scalar.copy(out=scale_row[:, 0, :].rearrange("p (n t) -> p n t", t=4), in_=spread[:].rearrange("p t n -> p n t"))
+        nc.scalar.copy(out=scale_row[:].rearrange("p (n t) -> p n t", t=4), in_=spread[:].rearrange("p t n -> p n t"))
 
         turned, k_first, x1_q, h_acc, h, h_q, x2_rows, sums = {}, {}, {}, {}, {}, {}, {}, {}
 
@@ -88,7 +85,7 @@ def tile_coattentionandcombine_pa_w4_kernel(tc, x1, w_words, w_scales, x2_bytes,
 
         def turn(name, i, rows):
             words = rows.bitcast(F32)
-            acc = psum.tile([P, 2, 2, P], F32, name=name + "_turned", tag=name + "_turned")
+            acc = psum.tile([P, 2, 2, P], F32, name=name + "_turned", tag=name + "_turned", bufs=BANKS[name])
             for c in range(2):
                 for u in range(2):
                     nc.tensor.transpose(acc[:, u, c, :], words[:, 256 * c + u : 256 * (c + 1) : 2], ident[:])
@@ -112,10 +109,9 @@ def tile_coattentionandcombine_pa_w4_kernel(tc, x1, w_words, w_scales, x2_bytes,
             if i == 0:
                 nc.vector.tensor_copy(out=w[:].rearrange("p (t m e) -> p t m e", t=4, e=2), in_=w_raw[:].rearrange("p (m t e) -> p t m e", t=4, e=2))
                 nc.gpsimd.tensor_copy(out=w_plane[:].rearrange("p (t m) -> p t m", t=4), in_=w_raw_plane[:].rearrange("p (m t) -> p t m", t=4))
-                nc.vector.tensor_copy(out=scale_row[:, 1, :], in_=scale_row[:, 0, :])
 
         def stage_T1(i):
-            turn("x1", i, x1_raw[i][:].rearrange("p c k -> p (c k)"))
+            turn("x1", i, half(x1_raw, i))
 
         def stage_C1(i):
             interleave("x1", i, "C1")
@@ -125,7 +121,9 @@ def tile_coattentionandcombine_pa_w4_kernel(tc, x1, w_words, w_scales, x2_bytes,
 
         def stage_P(i):
             rows = work.tile([P, 2 * D], BF16, name="x2_rows", tag="x2_rows")
-            nc.vector.tensor_tensor(out=rows[:], in0=x2_codes_in[i][:].bitcast(E4M3), in1=scale_row[:].rearrange("p c k -> p (c k)"), op=MULT)
+            for c in range(2):
+                cols = slice(D * c, D * (c + 1))
+                nc.vector.tensor_tensor(out=rows[:, cols], in0=half(x2_raw, i)[:, cols].bitcast(E4M3), in1=scale_row[:], op=MULT)
             x2_rows[i] = rows
 
         def stage_T2(i):
@@ -143,7 +141,7 @@ def tile_coattentionandcombine_pa_w4_kernel(tc, x1, w_words, w_scales, x2_bytes,
             words, plane = x1_q[i]
             for c in range(2):
                 rows = slice(P * c, P * (c + 1))
-                acc = psum.tile([P, 4, P], F32, name="h_acc", tag="h_acc")
+                acc = psum.tile([P, 4, P], F32, name="h_acc", tag="h_acc", bufs=BANKS["h"])
                 for t in range(4):
                     nc.tensor.matmul_mx(
                         out=acc[:, t, :],
@@ -179,7 +177,7 @@ def tile_coattentionandcombine_pa_w4_kernel(tc, x1, w_words, w_scales, x2_bytes,
             words, plane = h_q[i]
             for c in range(2):
                 rows = slice(P * c, P * (c + 1))
-                acc = psum.tile([P, L], F32, name="sim_acc", tag="sim_acc")
+                acc = psum.tile([P, L], F32, name="sim_acc", tag="sim_acc", bufs=BANKS["sim"])
                 nc.tensor.matmul_mx(
                     out=acc[:],
                     lhsT=words[:, rows].bitcast(FP8X4),
@@ -204,21 +202,21 @@ def tile_coattentionandcombine_pa_w4_kernel(tc, x1, w_words, w_scales, x2_bytes,
             sim_out(i, 1, "OC1")
 
         order = (
-            (stage_C2, 3),
-            (stage_P, 1),
-            (stage_H, 4),
-            (stage_HC0, 4),
             (stage_T1, 0),
-            (stage_O, 5),
-            (stage_T2, 2),
-            (stage_HC1, 4),
-            (stage_OC0, 5),
-            (stage_Q2, 3),
-            (stage_OC1, 5),
-            (stage_C1, 0),
+            (stage_HC0, 2),
+            (stage_HC1, 2),
             (stage_W, 0),
-            (stage_HQ, 4),
-            (stage_Q1, 2),
+            (stage_C1, 0),
+            (stage_P, 0),
+            (stage_T2, 1),
+            (stage_C2, 1),
+            (stage_OC1, 4),
+            (stage_O, 3),
+            (stage_H, 1),
+            (stage_OC0, 3),
+            (stage_HQ, 2),
+            (stage_Q1, 0),
+            (stage_Q2, 1),
         )
         for step in range(HALVES + max(lag for stage, lag in order)):
             for stage, lag in order:

@@ -18,8 +18,8 @@ FP4X4 = mybir.dt.float4_e2m1fn_x4
 MULT = mybir.AluOpType.mult
 
 HALVES = 2 * B
-BANKS = {"x1": 2, "x2": 1, "h": 2, "sim": 3}
-ON_VECTOR = (("C2", 3), ("HC1", 4), ("HC1", 5), ("OC1", 1), ("OC1", 2), ("OC1", 4))
+BANKS = {"x1": 1, "x2": 1, "h": 4, "sim": 2}
+ON_VECTOR = (("C2", 5), ("HC1", 2), ("HC1", 5), ("OC0", 2), ("OC1", 0))
 HROWS = 256
 
 
@@ -63,14 +63,14 @@ def tile_coattentionandcombine_pa_w4_kernel(tc, x1, w_words, w_scales, x2_bytes,
         nc.sync.dma_start(out=w_raw[:].bitcast(I32), in_=w_words.rearrange("g p n -> p (g n)").bitcast(I32))
         load(x2_raw, x2_view, 0, (0,))
         load(x1_raw, x1_view, 0, (0,))
-        load(x1_raw, x1_view, 0, (1,))
         for q in range(4):
             nc.sync.dma_start(out=w_raw_plane[32 * q : 32 * q + 4, :].bitcast(I32), in_=w_scales[0, 4 * q : 4 * q + 4, :].bitcast(I32))
+        load(x1_raw, x1_view, 0, (1,))
         load(x2_raw, x2_view, 0, (1,))
         load(x1_raw, x1_view, 1, (0, 1))
         load(x2_raw, x2_view, 1, (0, 1))
-        load(x1_raw, x1_view, 2, (0, 1))
         load(x2_raw, x2_view, 2, (0, 1))
+        load(x1_raw, x1_view, 2, (0, 1))
         make_identity(nc, ident[:])
 
         spread = psum.tile([P, 4, P], F32, name="spread", tag="x2_turned", bufs=BANKS["x2"])
@@ -108,7 +108,10 @@ def tile_coattentionandcombine_pa_w4_kernel(tc, x1, w_words, w_scales, x2_bytes,
         def stage_W(i):
             if i == 0:
                 nc.vector.tensor_copy(out=w[:].rearrange("p (t m e) -> p t m e", t=4, e=2), in_=w_raw[:].rearrange("p (m t e) -> p t m e", t=4, e=2))
-                nc.gpsimd.tensor_copy(out=w_plane[:].rearrange("p (t m) -> p t m", t=4), in_=w_raw_plane[:].rearrange("p (m t) -> p t m", t=4))
+
+        def stage_Wp(i):
+            if i == 0:
+                nc.vector.tensor_copy(out=w_plane[:].rearrange("p (t m) -> p t m", t=4), in_=w_raw_plane[:].rearrange("p (m t) -> p t m", t=4))
 
         def stage_T1(i):
             turn("x1", i, half(x1_raw, i))
@@ -202,21 +205,22 @@ def tile_coattentionandcombine_pa_w4_kernel(tc, x1, w_words, w_scales, x2_bytes,
             sim_out(i, 1, "OC1")
 
         order = (
-            (stage_T1, 0),
             (stage_HC0, 2),
+            (stage_OC1, 4),
             (stage_HC1, 2),
             (stage_W, 0),
-            (stage_C1, 0),
-            (stage_P, 0),
+            (stage_T1, 0),
             (stage_T2, 1),
-            (stage_C2, 1),
-            (stage_OC1, 4),
+            (stage_P, 0),
             (stage_O, 3),
+            (stage_C1, 0),
+            (stage_Wp, 0),
             (stage_H, 1),
-            (stage_OC0, 3),
+            (stage_C2, 1),
             (stage_HQ, 2),
-            (stage_Q1, 0),
+            (stage_OC0, 3),
             (stage_Q2, 1),
+            (stage_Q1, 0),
         )
         for step in range(HALVES + max(lag for stage, lag in order)):
             for stage, lag in order:

@@ -18,8 +18,9 @@ FP4X4 = mybir.dt.float4_e2m1fn_x4
 MULT = mybir.AluOpType.mult
 
 HALVES = 2 * B
-BANKS = {"x1": 1, "x2": 1, "h": 4, "sim": 2}
-ON_VECTOR = (("C2", 5), ("HC1", 2), ("HC1", 5), ("OC0", 2), ("OC1", 0))
+FILL = {0: 2, 1: 1, 2: 2}
+BANKS = {"x1": 1, "x2": 2, "h": 2, "sim": 3}
+ON_VECTOR = (("C2", 3), ("C2", 5), ("HC0", 2), ("HC0", 3), ("HC1", 5), ("OC0", 5), ("OC1", 4),)
 HROWS = 256
 
 
@@ -43,6 +44,7 @@ def tile_coattentionandcombine_pa_w4_kernel(tc, x1, w_words, w_scales, x2_bytes,
         w_plane = keep.tile([P, D], U8, name="w_plane", align_bytes=64)
         ident = keep.tile([P, P], F32, name="ident")
         warm = keep.tile([P, 2], F32, name="warm")
+        zeros = keep.tile([P, P], F32, name="zeros")
 
         x1_view = x1.rearrange("b (p c) k -> b p (c k)", c=4)
         x2_view = x2_bytes.rearrange("b (p c) k -> b p (c k)", c=4)
@@ -57,21 +59,30 @@ def tile_coattentionandcombine_pa_w4_kernel(tc, x1, w_words, w_scales, x2_bytes,
             return tiles[b][:, 2 * D * j : 2 * D * (j + 1)]
 
         nc.vector.memset(w_raw_plane[:].bitcast(I32), 0)
+        nc.vector.memset(zeros[:], 0.0)
         nc.vector.memset(warm[:], 0.0)
         nc.scalar.dma_start(out=scale_col[:], in_=x2_scale.rearrange("a o (p t) -> p (a o t)", t=4))
         nc.scalar.copy(out=warm[:, 0:1], in_=warm[:, 1:2])
         nc.sync.dma_start(out=w_raw[:].bitcast(I32), in_=w_words.rearrange("g p n -> p (g n)").bitcast(I32))
-        load(x2_raw, x2_view, 0, (0,))
         load(x1_raw, x1_view, 0, (0,))
+        load(x2_raw, x2_view, 0, (0,))
+        load(x1_raw, x1_view, 0, (1,))
         for q in range(4):
             nc.sync.dma_start(out=w_raw_plane[32 * q : 32 * q + 4, :].bitcast(I32), in_=w_scales[0, 4 * q : 4 * q + 4, :].bitcast(I32))
-        load(x1_raw, x1_view, 0, (1,))
         load(x2_raw, x2_view, 0, (1,))
-        load(x1_raw, x1_view, 1, (0, 1))
         load(x2_raw, x2_view, 1, (0, 1))
+        load(x1_raw, x1_view, 1, (0, 1))
         load(x2_raw, x2_view, 2, (0, 1))
         load(x1_raw, x1_view, 2, (0, 1))
         make_identity(nc, ident[:])
+
+        idle = psum.tile([P, P], F32, name="idle", tag="sim_acc", bufs=BANKS["sim"])
+
+        def busy(count):
+            for k in range(count):
+                nc.tensor.matmul(out=idle[:], lhsT=zeros[:], rhs=zeros[:], start=True, stop=True)
+
+        busy(4)
 
         spread = psum.tile([P, 4, P], F32, name="spread", tag="x2_turned", bufs=BANKS["x2"])
         for t in range(4):
@@ -175,6 +186,9 @@ def tile_coattentionandcombine_pa_w4_kernel(tc, x1, w_words, w_scales, x2_bytes,
         def stage_HQ(i):
             h_q[i] = quantize(h[i], "h")
 
+        def stage_K(i):
+            busy(FILL.get(i, 0))
+
         def stage_O(i):
             b = i // 2
             words, plane = h_q[i]
@@ -205,22 +219,23 @@ def tile_coattentionandcombine_pa_w4_kernel(tc, x1, w_words, w_scales, x2_bytes,
             sim_out(i, 1, "OC1")
 
         order = (
-            (stage_HC0, 2),
-            (stage_OC1, 4),
-            (stage_HC1, 2),
-            (stage_W, 0),
             (stage_T1, 0),
-            (stage_T2, 1),
+            (stage_HC0, 2),
+            (stage_W, 0),
+            (stage_OC1, 4),
             (stage_P, 0),
-            (stage_O, 3),
+            (stage_HC1, 2),
             (stage_C1, 0),
             (stage_Wp, 0),
-            (stage_H, 1),
+            (stage_T2, 1),
+            (stage_K, 0),
+            (stage_O, 3),
             (stage_C2, 1),
+            (stage_H, 1),
             (stage_HQ, 2),
-            (stage_OC0, 3),
-            (stage_Q2, 1),
             (stage_Q1, 0),
+            (stage_Q2, 1),
+            (stage_OC0, 3),
         )
         for step in range(HALVES + max(lag for stage, lag in order)):
             for stage, lag in order:

from contextlib import ExitStack

import concourse.mybir as mybir
from concourse.masks import make_identity

B, L, D = 3, 512, 512
P = 128
FLOPS = 2 * 2 * B * L * L * D

F32 = mybir.dt.float32
BF16 = mybir.dt.bfloat16
I32 = mybir.dt.int32
U32 = mybir.dt.uint32
U8 = mybir.dt.uint8
E4M3 = mybir.dt.float8_e4m3fn
FP8X4 = mybir.dt.float8_e4m3fn_x4
FP4X4 = mybir.dt.float4_e2m1fn_x4
MULT = mybir.AluOpType.mult

HALVES = 2 * B
FILL = {0: 2, 1: 1, 2: 2}
BANKS = {"x1": 1, "x2": 2, "h": 2, "sim": 3}
ON_VECTOR = (("C2", 3), ("C2", 5), ("HC0", 2), ("HC0", 3), ("HC1", 5), ("OC0", 5), ("OC1", 4),)
HROWS = 256


def tile_coattentionandcombine_pa_w4_kernel(tc, x1, w_words, w_scales, x2_bytes, x2_scale, out):
    nc = tc.nc
    with ExitStack() as ctx:
        keep = ctx.enter_context(tc.tile_pool(name="keep", bufs=1))
        work = ctx.enter_context(tc.tile_pool(name="work", bufs=6))
        psum = ctx.enter_context(tc.psum_pool(name="psum", bufs=2))
        ctx.enter_context(tc.manual_schedule())

        x1_raw = [keep.tile([P, 4 * D], BF16, name="x1_raw%d" % b) for b in range(B)]
        x2_raw = [keep.tile([P, 4 * D], U8, name="x2_raw%d" % b) for b in range(B)]
        x2_words = [keep.tile([P, L], U32, name="x2_words%d" % b, align_bytes=64) for b in range(B)]
        x2_planes = [keep.tile([P, L], U8, name="x2_planes%d" % b, align_bytes=64) for b in range(B)]
        scale_col = keep.tile([P, 4], F32, name="scale_col")
        scale_row = keep.tile([P, D], F32, name="scale_row")
        w_raw = keep.tile([P, 2 * D], U8, name="w_raw", align_bytes=64)
        w_raw_plane = keep.tile([P, D], U8, name="w_raw_plane", align_bytes=64)
        w = keep.tile([P, 2 * D], U8, name="w", align_bytes=64)
        w_plane = keep.tile([P, D], U8, name="w_plane", align_bytes=64)
        ident = keep.tile([P, P], F32, name="ident")
        warm = keep.tile([P, 2], F32, name="warm")
        zeros = keep.tile([P, P], F32, name="zeros")

        x1_view = x1.rearrange("b (p c) k -> b p (c k)", c=4)
        x2_view = x2_bytes.rearrange("b (p c) k -> b p (c k)", c=4)
        out_view = out.rearrange("b (p c) n -> b p c n", c=4)

        def load(tiles, view, b, halves):
            cols = slice(2 * D * halves[0], 2 * D * (halves[-1] + 1))
            nc.sync.dma_start(out=tiles[b][:, cols], in_=view[b, :, cols])

        def half(tiles, i):
            b, j = divmod(i, 2)
            return tiles[b][:, 2 * D * j : 2 * D * (j + 1)]

        nc.vector.memset(w_raw_plane[:].bitcast(I32), 0)
        nc.vector.memset(zeros[:], 0.0)
        nc.vector.memset(warm[:], 0.0)
        nc.scalar.dma_start(out=scale_col[:], in_=x2_scale.rearrange("a o (p t) -> p (a o t)", t=4))
        nc.scalar.copy(out=warm[:, 0:1], in_=warm[:, 1:2])
        nc.sync.dma_start(out=w_raw[:].bitcast(I32), in_=w_words.rearrange("g p n -> p (g n)").bitcast(I32))
        load(x1_raw, x1_view, 0, (0,))
        load(x2_raw, x2_view, 0, (0,))
        load(x1_raw, x1_view, 0, (1,))
        for q in range(4):
            nc.sync.dma_start(out=w_raw_plane[32 * q : 32 * q + 4, :].bitcast(I32), in_=w_scales[0, 4 * q : 4 * q + 4, :].bitcast(I32))
        load(x2_raw, x2_view, 0, (1,))
        load(x2_raw, x2_view, 1, (0, 1))
        load(x1_raw, x1_view, 1, (0, 1))
        load(x2_raw, x2_view, 2, (0, 1))
        load(x1_raw, x1_view, 2, (0, 1))
        make_identity(nc, ident[:])

        idle = psum.tile([P, P], F32, name="idle", tag="sim_acc", bufs=BANKS["sim"])

        def busy(count):
            for k in range(count):
                nc.tensor.matmul(out=idle[:], lhsT=zeros[:], rhs=zeros[:], start=True, stop=True)

        busy(4)

        spread = psum.tile([P, 4, P], F32, name="spread", tag="x2_turned", bufs=BANKS["x2"])
        for t in range(4):
            nc.tensor.transpose(spread[:, t, :], scale_col[:, t : t + 1].to_broadcast([P, P]), ident[:])
        nc.scalar.copy(out=scale_row[:].rearrange("p (n t) -> p n t", t=4), in_=spread[:].rearrange("p t n -> p n t"))

        turned, k_first, x1_q, h_acc, h, h_q, x2_rows, sums = {}, {}, {}, {}, {}, {}, {}, {}

        def fits(name, i):
            return nc.vector.tensor_copy if (name, i) in ON_VECTOR else nc.scalar.copy

        def turn(name, i, rows):
            words = rows.bitcast(F32)
            acc = psum.tile([P, 2, 2, P], F32, name=name + "_turned", tag=name + "_turned", bufs=BANKS[name])
            for c in range(2):
                for u in range(2):
                    nc.tensor.transpose(acc[:, u, c, :], words[:, 256 * c + u : 256 * (c + 1) : 2], ident[:])
            turned[name, i] = acc

        def interleave(name, i, stage):
            out_tile = work.tile([P, HROWS * 4], BF16, name=name + "_k", tag=name + "_k", align_bytes=64)
            fits(stage, i)(
                out=out_tile[:].bitcast(F32).rearrange("p (r u) -> p r u", u=2),
                in_=turned[name, i][:].rearrange("p u c r -> p (c r) u"),
            )
            k_first[name, i] = out_tile

        def quantize(rows, name):
            words = work.tile([P, HROWS], U32, name=name + "_w", tag=name + "_w", align_bytes=64)
            plane = work.tile([P, HROWS], U8, name=name + "_s", tag=name + "_s", align_bytes=64)
            nc.vector.quantize_mx(out=words[:].bitcast(FP8X4), scales=plane[:], in_=rows[:])
            return words, plane

        def stage_W(i):
            if i == 0:
                nc.vector.tensor_copy(out=w[:].rearrange("p (t m e) -> p t m e", t=4, e=2), in_=w_raw[:].rearrange("p (m t e) -> p t m e", t=4, e=2))

        def stage_Wp(i):
            if i == 0:
                nc.vector.tensor_copy(out=w_plane[:].rearrange("p (t m) -> p t m", t=4), in_=w_raw_plane[:].rearrange("p (m t) -> p t m", t=4))

        def stage_T1(i):
            turn("x1", i, half(x1_raw, i))

        def stage_C1(i):
            interleave("x1", i, "C1")

        def stage_Q1(i):
            x1_q[i] = quantize(k_first["x1", i], "x1")

        def stage_P(i):
            rows = work.tile([P, 2 * D], BF16, name="x2_rows", tag="x2_rows")
            for c in range(2):
                cols = slice(D * c, D * (c + 1))
                nc.vector.tensor_tensor(out=rows[:, cols], in0=half(x2_raw, i)[:, cols].bitcast(E4M3), in1=scale_row[:], op=MULT)
            x2_rows[i] = rows

        def stage_T2(i):
            turn("x2", i, x2_rows[i][:])

        def stage_C2(i):
            interleave("x2", i, "C2")

        def stage_Q2(i):
            b, j = divmod(i, 2)
            cols = slice(HROWS * j, HROWS * (j + 1))
            nc.vector.quantize_mx(out=x2_words[b][:, cols].bitcast(FP8X4), scales=x2_planes[b][:, cols], in_=k_first["x2", i][:])

        def stage_H(i):
            words, plane = x1_q[i]
            for c in range(2):
                rows = slice(P * c, P * (c + 1))
                acc = psum.tile([P, 4, P], F32, name="h_acc", tag="h_acc", bufs=BANKS["h"])
                for t in range(4):
                    nc.tensor.matmul_mx(
                        out=acc[:, t, :],
                        lhsT=w[:, 256 * t : 256 * (t + 1)].bitcast(FP4X4),
                        lhsT_scale=w_plane[:, P * t : P * (t + 1)],
                        rhs=words[:, rows].bitcast(FP8X4),
                        rhs_scale=plane[:, rows],
                        start=True,
                        stop=True,
                    )
                h_acc[i, c] = acc

        def h_out(i, c, stage):
            if c == 0:
                h_tile = work.tile([P, HROWS * 4], BF16, name="h", tag="h", align_bytes=64)
                h[i] = h_tile
            fits(stage, i)(
                out=h[i][:, 512 * c : 512 * (c + 1)].rearrange("p (r t) -> p r t", t=4),
                in_=h_acc[i, c][:].rearrange("p t r -> p r t"),
            )

        def stage_HC0(i):
            h_out(i, 0, "HC0")

        def stage_HC1(i):
            h_out(i, 1, "HC1")

        def stage_HQ(i):
            h_q[i] = quantize(h[i], "h")

        def stage_K(i):
            busy(FILL.get(i, 0))

        def stage_O(i):
            b = i // 2
            words, plane = h_q[i]
            for c in range(2):
                rows = slice(P * c, P * (c + 1))
                acc = psum.tile([P, L], F32, name="sim_acc", tag="sim_acc", bufs=BANKS["sim"])
                nc.tensor.matmul_mx(
                    out=acc[:],
                    lhsT=words[:, rows].bitcast(FP8X4),
                    lhsT_scale=plane[:, rows],
                    rhs=x2_words[b][:].bitcast(FP8X4),
                    rhs_scale=x2_planes[b][:],
                    start=True,
                    stop=True,
                )
                sums[i, c] = acc

        def sim_out(i, c, stage):
            b, j = divmod(i, 2)
            result = work.tile([P, L], F32, name="result", tag="result", bufs=12)
            fits(stage, i)(out=result[:].rearrange("p (m c) -> p m c", c=4), in_=sums[i, c][:].rearrange("p (c m) -> p m c", c=4))
            nc.sync.dma_start(out=out_view[b, :, 2 * j + c, :], in_=result[:])

        def stage_OC0(i):
            sim_out(i, 0, "OC0")

        def stage_OC1(i):
            sim_out(i, 1, "OC1")

        order = (
            (stage_T1, 0),
            (stage_HC0, 2),
            (stage_W, 0),
            (stage_OC1, 4),
            (stage_P, 0),
            (stage_HC1, 2),
            (stage_C1, 0),
            (stage_Wp, 0),
            (stage_T2, 1),
            (stage_K, 0),
            (stage_O, 3),
            (stage_C2, 1),
            (stage_H, 1),
            (stage_HQ, 2),
            (stage_Q1, 0),
            (stage_Q2, 1),
            (stage_OC0, 3),
        )
        for step in range(HALVES + max(lag for stage, lag in order)):
            for stage, lag in order:
                if 0 <= step - lag < HALVES:
                    stage(step - lag)
